import numpy as np
import ml_dtypes


def mxq(x, axis, fmt="e4m3"):
    dtype, down = {"e4m3": (ml_dtypes.float8_e4m3fn, 7), "e5m2": (ml_dtypes.float8_e5m2, 14)}[fmt]
    v = np.moveaxis(np.asarray(x, np.float32).astype(ml_dtypes.bfloat16).astype(np.float64), axis, -1)
    blocks = v.reshape(v.shape[:-1] + (-1, 32))
    amax = np.abs(blocks).max(-1, keepdims=True)
    byte = np.maximum(np.where(amax > 0, np.frexp(amax)[1] - 1 + 127, 0) - down, 1)
    scale = np.exp2(byte - 127.0)
    codes = (blocks / scale).astype(np.float32).astype(dtype).astype(np.float64)
    return np.moveaxis((codes * scale).reshape(v.shape), -1, axis)


WIDE = False


def mx_kscale(k):
    if not WIDE:
        return np.ones(k)
    levels = np.array([30, -30])
    if k % 512:
        return np.exp2(np.random.permutation(np.resize(levels, k // 32))).repeat(32)
    a = np.empty((k // 512, 16))
    for p in range(k // 512):
        a[p, :8] = np.random.permutation(np.resize(levels, 8))
        for g in range(8):
            far = levels[np.abs(levels - a[p, g]) >= 10]
            a[p, g + 8] = far[np.random.randint(len(far))]
    return np.exp2(a.ravel()).repeat(32)


BF16 = ml_dtypes.bfloat16


def bf(x):
    return np.asarray(x, np.float32).astype(BF16)


def f64(x):
    return np.asarray(x).astype(np.float64)


B, S, H, NH, NKV, HD = 2, 512, 2048, 16, 4, 128
EPS = 1e-6


def rms_norm(x, w):
    var = np.mean(x * x, axis=-1, keepdims=True)
    return x * (1.0 / np.sqrt(var + EPS)) * w


def rotate_half(x):
    x1, x2 = np.split(x, 2, axis=-1)
    return np.concatenate([-x2, x1], axis=-1)


def setup_inputs():
    s = mx_kscale(H)
    inv_freq = 1.0 / (10000.0 ** (np.arange(0, HD, 2) / HD))
    freqs = np.arange(S)[:, None] * inv_freq[None, :]
    emb = np.concatenate([freqs, freqs], axis=-1)
    return {"hidden_states": bf(np.random.standard_normal((B, S, H)) * s),
            "cos": bf(np.cos(emb)),
            "sin": bf(np.sin(emb)),
            "wq": bf(np.random.standard_normal((NH * HD, H)) / np.sqrt(H) / s[None, :]),
            "wk": bf(np.random.standard_normal((NKV * HD, H)) / np.sqrt(H) / s[None, :]),
            "q_norm_w": bf(1.0 + 0.1 * np.random.standard_normal(HD)),
            "k_norm_w": bf(1.0 + 0.1 * np.random.standard_normal(HD)),
            "ssmax_scale": bf((1.0 + 0.2 * np.random.standard_normal((1, NH, 1, 1))) / np.log(S))}


def reference(hidden_states, cos, sin, wq, wk, q_norm_w, k_norm_w, ssmax_scale):
    xq = mxq(f64(hidden_states), 2, "e5m2")
    q = (xq @ mxq(f64(wq), 1, "e4m3").T).reshape(B, S, NH, HD)
    k = (xq @ mxq(f64(wk), 1, "e4m3").T).reshape(B, S, NKV, HD)
    q = rms_norm(q, f64(q_norm_w)).transpose(0, 2, 1, 3)
    k = rms_norm(k, f64(k_norm_w)).transpose(0, 2, 1, 3)
    c = f64(cos)[None, None]
    sn = f64(sin)[None, None]
    q = q * c + rotate_half(q) * sn
    k = k * c + rotate_half(k) * sn
    q = q * (f64(ssmax_scale) * np.log(S))
    return q, k

@@ -1,0 +1,259 @@
+import math
+from contextlib import ExitStack
+
+import concourse.mybir as mybir
+from concourse.masks import make_identity
+
+B, S, H, NH, NKV, HD = 2, 512, 2048, 16, 4, 128
+EPS = 1e-6
+FLOPS = 2 * B * S * H * (NH + NKV) * HD
+
+F32 = mybir.dt.float32
+BF16 = mybir.dt.bfloat16
+U32 = mybir.dt.uint32
+U8 = mybir.dt.uint8
+E5M2 = mybir.dt.float8_e5m2_x4
+E4M3 = mybir.dt.float8_e4m3fn_x4
+ALU = mybir.AluOpType
+ACT = mybir.ActivationFunctionType
+
+P = 128
+HALF = HD // 2
+PASSES = H // 512
+HEADS = 4
+ROWS = S // P
+TOK_TILES = B * ROWS
+SWEEPS = (NH + NKV) // HEADS
+Q_SWEEPS = NH // HEADS
+TILES = SWEEPS * TOK_TILES
+SLOT_WORDS = 256
+
+
+def tile_biboattention_pa_kernel(
+    tc, hidden_states, cos, sin, wq, wk, q_norm_w, k_norm_w, ssmax_scale, out_0, out_1
+):
+    nc = tc.nc
+    with ExitStack() as ctx:
+        keep = ctx.enter_context(tc.tile_pool(name="keep", bufs=1))
+        work = ctx.enter_context(tc.tile_pool(name="work", bufs=3))
+        psum = ctx.enter_context(tc.psum_pool(name="psum", bufs=4))
+        ctx.enter_context(tc.manual_schedule())
+
+        ident = keep.tile([P, P], F32, name="ident")
+        make_identity(nc, ident[:])
+        ones = keep.tile([P, P], BF16, name="ones")
+        vec = keep.tile([P, 2 * HD + NH], BF16, name="vec")
+        nc.vector.memset(vec[:], 0.0)
+        nc.vector.memset(ones[:], 1.0)
+        nc.scalar.dma_start(out=vec[0:1, 0:HD], in_=q_norm_w.rearrange("(o d) -> o d", o=1))
+        nc.scalar.dma_start(out=vec[0:1, HD : 2 * HD], in_=k_norm_w.rearrange("(o d) -> o d", o=1))
+        nc.scalar.dma_start(out=vec[0:1, 2 * HD :], in_=ssmax_scale.rearrange("o h a c -> o (h a c)"))
+
+        raw, staged, codes, scales = {}, {}, {}, {}
+
+        def load(unit):
+            kind, a, g = unit
+            tile = keep.tile([P, 4, 512], BF16, name="raw_%s%d_%d" % unit)
+            if kind == "x":
+                src = hidden_states[a // ROWS].rearrange("(p i) (g k) -> p i g k", i=ROWS, k=512)[:, a % ROWS]
+            else:
+                w = wq[512 * a : 512 * (a + 1)] if a < Q_SWEEPS else wk
+                src = w[:, 512 * g : 512 * (g + 1)].rearrange("(r p) k -> p r k", p=P)
+            if unit == ("x", 0, 0):
+                nc.sync.dma_start(out=tile[:, 0:2], in_=src[:, 0:2])
+                nc.sync.dma_start(out=tile[:, 2:4], in_=src[:, 2:4])
+            else:
+                nc.sync.dma_start(out=tile[:], in_=src)
+            raw[unit] = tile
+
+        def transpose_and_stage(units, between=None):
+            banks = []
+            for unit in units:
+                words = raw[unit][:].rearrange("p a k -> p (a k)").bitcast(F32)
+                for pair in range(2):
+                    bank = psum.tile([P, 2, 2, P], F32, name="tr", tag="tr")
+                    for a in range(2):
+                        base = SLOT_WORDS * (2 * pair + a)
+                        for u in range(2):
+                            nc.tensor.transpose(bank[:, a, u, :], words[:, base + u : base + SLOT_WORDS : 2], ident[:])
+                    banks.append((unit, pair, bank))
+            if between is not None:
+                between()
+            for unit, pair, bank in banks:
+                if pair == 0:
+                    staged[unit] = work.tile([P, 4 * 512], BF16, name="staged", tag="staged", bufs=4, align_bytes=64)
+                dst = staged[unit][:].bitcast(F32).rearrange("p (a c u) -> p a c u", a=4, u=2)
+                nc.scalar.copy(out=dst[:, 2 * pair : 2 * pair + 2], in_=bank[:].rearrange("p a u c -> p a c u"))
+
+        def quantize(unit):
+            if unit[0] == "x":
+                codes[unit] = keep.tile([P, 512], U32, name="xc%d" % unit[1], align_bytes=64)
+                scales[unit] = keep.tile([P, 512], U8, name="xs%d" % unit[1], align_bytes=64)
+                fmt = E5M2
+            else:
+                codes[unit] = work.tile([P, 512], U32, name="wc", tag="wc", bufs=2 * PASSES, align_bytes=64)
+                scales[unit] = work.tile([P, 512], U8, name="ws", tag="ws", bufs=2 * PASSES, align_bytes=64)
+                fmt = E4M3
+            nc.vector.quantize_mx(out=codes[unit][:].bitcast(fmt), scales=scales[unit][:], in_=staged[unit][:])
+
+        acc = {}
+
+        def multiply(t):
+            sweep, tok = divmod(t, TOK_TILES)
+            acc[t] = psum.tile([P, 512], F32, name="acc", tag="acc")
+            x = ("x", tok, 0)
+            for g in range(PASSES):
+                w = ("w", sweep, g)
+                cols = slice(P * g, P * (g + 1))
+                nc.tensor.matmul_mx(
+                    out=acc[t][:],
+                    lhsT=codes[x][:, cols].bitcast(E5M2),
+                    lhsT_scale=scales[x][:, cols],
+                    rhs=codes[w][:].bitcast(E4M3),
+                    rhs_scale=scales[w][:],
+                    start=(g == 0),
+                    stop=(g == PASSES - 1),
+                )
+
+        sumsq = keep.tile([P, TILES, HEADS], F32, name="sumsq")
+        rstd_gain = keep.tile([P, Q_SWEEPS, TOK_TILES, HEADS, 2], F32, name="rstd_gain")
+        factor = keep.tile([P, TILES, HEADS], F32, name="factor")
+
+        def norm_stats(t):
+            sweep, tok = divmod(t, TOK_TILES)
+            squares = work.tile([P, HEADS, HD], BF16, name="squares", tag="squares")
+            for h in range(HEADS):
+                nc.scalar.activation(
+                    out=squares[:, h, :],
+                    in_=acc[t][:, HD * h : HD * (h + 1)],
+                    func=ACT.Square,
+                    accum_out=sumsq[:, t, h : h + 1],
+                )
+            dst = rstd_gain[:, sweep, tok, :, 0] if sweep < Q_SWEEPS else factor[:, t, :]
+            nc.scalar.activation(out=dst, in_=sumsq[:, t, :], func=ACT.Abs_reciprocal_sqrt, scale=1.0 / HD, bias=EPS)
+
+        def apply_gain(t):
+            sweep, tok = divmod(t, TOK_TILES)
+            if sweep < Q_SWEEPS:
+                nc.vector.tensor_reduce(
+                    out=factor[:, t, :], in_=rstd_gain[:, sweep, tok], axis=mybir.AxisListType.X, op=ALU.mult
+                )
+
+        terms = {}
+
+        def rope_terms(t, h):
+            sweep, tok = divmod(t, TOK_TILES)
+            if h == 0:
+                terms[t] = work.tile([P, HEADS, 2, HD], F32, name="terms", tag="terms", bufs=4)
+            table = tables[0 if sweep < Q_SWEEPS else 1]
+            nc.vector.scalar_tensor_tensor(
+                out=terms[t][:, h],
+                in0=acc[t][:, HD * h : HD * (h + 1)].unsqueeze(1).to_broadcast([P, 2, HD]),
+                scalar=factor[:, t, h : h + 1],
+                in1=table[:, tok % ROWS],
+                op0=ALU.mult,
+                op1=ALU.mult,
+            )
+
+        result = {}
+
+        def rope_sum_and_store(t):
+            sweep, tok = divmod(t, TOK_TILES)
+            b, i = divmod(tok, ROWS)
+            if i == 0:
+                result[t // ROWS] = work.tile([P, HEADS, ROWS, HD], F32, name="result", tag="result")
+            res = result[t // ROWS]
+            engine = nc.vector if t == TILES - 1 else nc.gpsimd
+            for half in range(2):
+                own = slice(HALF * half, HALF * (half + 1))
+                other = slice(HALF * (1 - half), HALF * (2 - half))
+                engine.tensor_tensor(
+                    out=res[:, :, i, own], in0=terms[t][:, :, 0, own], in1=terms[t][:, :, 1, other], op=ALU.add
+                )
+            heads = out_0[b, HEADS * sweep : HEADS * (sweep + 1)] if sweep < Q_SWEEPS else out_1[b]
+            dst = heads.rearrange("h (p i) d -> p h i d", i=ROWS)
+            if t >= TILES - ROWS:
+                nc.sync.dma_start(out=dst[:, :, i], in_=res[:, :, i])
+            elif i == ROWS - 1:
+                nc.sync.dma_start(out=dst, in_=res[:])
+
+        xs = [("x", a, 0) for a in range(TOK_TILES)]
+        ws = [[("w", j, g) for g in range(PASSES)] for j in range(SWEEPS)]
+        head = [xs[0]] + ws[0] + xs[1:3]
+        after = {t: [] for t in range(-1, TILES)}
+        for n, unit in enumerate(xs[3:]):
+            after[n].append(unit)
+        for g, t in enumerate((0, 2, 4, 5)):
+            after[t].append(ws[1][g])
+        for j in range(2, SWEEPS):
+            for g in range(PASSES):
+                after[TOK_TILES * (j - 1) - 1 + 2 * g].append(ws[j][g])
+
+        for unit in head:
+            load(unit)
+        cos_sb = keep.tile([P, ROWS, HD], BF16, name="cos_sb")
+        sin_sb = keep.tile([P, ROWS, HD], BF16, name="sin_sb")
+        nc.sync.dma_start(out=cos_sb[:], in_=cos.rearrange("(p i) d -> p i d", i=ROWS))
+        nc.sync.dma_start(out=sin_sb[:], in_=sin.rearrange("(p i) d -> p i d", i=ROWS))
+        for t in range(TILES):
+            for unit in after[t]:
+                load(unit)
+
+        for unit in head:
+            transpose_and_stage([unit])
+            quantize(unit)
+
+        spread = psum.tile([P, 512], F32, name="spread", tag="acc")
+        nc.tensor.matmul(out=spread[:, 0 : 2 * HD + NH], lhsT=ones[:], rhs=vec[:], start=True, stop=True)
+        tables = [keep.tile([P, ROWS, 2, HD], F32, name="table%d" % n) for n in range(2)]
+
+        def build_table(n):
+            w = spread[:, HD * n : HD * (n + 1)].unsqueeze(1)
+            nc.vector.tensor_tensor(
+                out=tables[n][:, :, 0, :], in0=cos_sb[:], in1=w.to_broadcast([P, ROWS, HD]), op=ALU.mult
+            )
+            nc.vector.tensor_tensor(
+                out=tables[n][:, :, 1, 0:HALF],
+                in0=sin_sb[:, :, HALF:HD],
+                in1=w[:, :, 0:HALF].to_broadcast([P, ROWS, HALF]),
+                op=ALU.mult,
+            )
+            nc.vector.scalar_tensor_tensor(
+                out=tables[n][:, :, 1, HALF:HD],
+                in0=sin_sb[:, :, 0:HALF],
+                scalar=-1.0,
+                in1=w[:, :, HALF:HD].to_broadcast([P, ROWS, HALF]),
+                op0=ALU.mult,
+                op1=ALU.mult,
+            )
+
+        gain = spread[:, 2 * HD : 2 * HD + NH].rearrange("p (j h) -> p j h", h=HEADS).unsqueeze(2)
+        nc.vector.tensor_scalar(
+            out=rstd_gain[:, :, :, :, 1],
+            in0=gain.to_broadcast([P, Q_SWEEPS, TOK_TILES, HEADS]),
+            scalar1=math.log(S),
+            scalar2=None,
+            op0=ALU.mult,
+        )
+        build_table(0)
+
+        def start_tile(t):
+            multiply(t)
+            transpose_and_stage(after[t], between=lambda: norm_stats(t))
+
+        start_tile(0)
+        apply_gain(0)
+        build_table(1)
+        for t in range(TILES):
+            more = t + 1 < TILES
+            if more:
+                start_tile(t + 1)
+            for h in range(HEADS):
+                if more and h == HEADS - 1 and not after[t]:
+                    apply_gain(t + 1)
+                rope_terms(t, h)
+            rope_sum_and_store(t)
+            if more and after[t]:
+                apply_gain(t + 1)
+                for unit in after[t]:
+                    quantize(unit)

@@ -26,6 +26,11 @@ TOK_TILES = B * ROWS
 SWEEPS = (NH + NKV) // HEADS
 Q_SWEEPS = NH // HEADS
 TILES = SWEEPS * TOK_TILES
+BANKS = {"acc": 6, "tr": 2}
+LAST_STEP = 4
+HEAD_SWEEPS = 3
+W_BUFS = 12
+RAW_BUFS = 22
 SLOT_WORDS = 256
 
 
@@ -53,12 +58,15 @@ def tile_biboattention_pa_kernel(
 
         def load(unit):
             kind, a, g = unit
-            tile = keep.tile([P, 4, 512], BF16, name="raw_%s%d_%d" % unit)
+            tile = work.tile([P, 4, 512], BF16, name="raw", tag="raw", bufs=RAW_BUFS)
             if kind == "x":
                 src = hidden_states[a // ROWS].rearrange("(p i) (g k) -> p i g k", i=ROWS, k=512)[:, a % ROWS]
             else:
                 w = wq[512 * a : 512 * (a + 1)] if a < Q_SWEEPS else wk
-                src = w[:, 512 * g : 512 * (g + 1)].rearrange("(r p) k -> p r k", p=P)
+                if a < HEAD_SWEEPS:
+                    src = w[P * g : P * (g + 1)].rearrange("p (g k) -> p g k", k=512)
+                else:
+                    src = w[:, 512 * g : 512 * (g + 1)].rearrange("(r p) k -> p r k", p=P)
             if unit == ("x", 0, 0):
                 nc.sync.dma_start(out=tile[:, 0:2], in_=src[:, 0:2])
                 nc.sync.dma_start(out=tile[:, 2:4], in_=src[:, 2:4])
@@ -66,12 +74,12 @@ def tile_biboattention_pa_kernel(
                 nc.sync.dma_start(out=tile[:], in_=src)
             raw[unit] = tile
 
-        def transpose_and_stage(units, between=None):
+        def transpose_and_stage(units, between=None, tag="tr"):
             banks = []
             for unit in units:
                 words = raw[unit][:].rearrange("p a k -> p (a k)").bitcast(F32)
                 for pair in range(2):
-                    bank = psum.tile([P, 2, 2, P], F32, name="tr", tag="tr")
+                    bank = psum.tile([P, 2, 2, P], F32, name="tr", tag=tag, bufs=BANKS[tag])
                     for a in range(2):
                         base = SLOT_WORDS * (2 * pair + a)
                         for u in range(2):
@@ -89,18 +97,23 @@ def tile_biboattention_pa_kernel(
             if unit[0] == "x":
                 codes[unit] = keep.tile([P, 512], U32, name="xc%d" % unit[1], align_bytes=64)
                 scales[unit] = keep.tile([P, 512], U8, name="xs%d" % unit[1], align_bytes=64)
-                fmt = E5M2
-            else:
-                codes[unit] = work.tile([P, 512], U32, name="wc", tag="wc", bufs=2 * PASSES, align_bytes=64)
-                scales[unit] = work.tile([P, 512], U8, name="ws", tag="ws", bufs=2 * PASSES, align_bytes=64)
-                fmt = E4M3
-            nc.vector.quantize_mx(out=codes[unit][:].bitcast(fmt), scales=scales[unit][:], in_=staged[unit][:])
+                nc.vector.quantize_mx(out=codes[unit][:].bitcast(E5M2), scales=scales[unit][:], in_=staged[unit][:])
+                return
+            by_rows = unit[1] < HEAD_SWEEPS
+            for g in range(PASSES) if by_rows else [unit[2]]:
+                key = ("w", unit[1], g)
+                if key not in codes:
+                    codes[key] = work.tile([P, 512], U32, name="wc", tag="wc", bufs=W_BUFS, align_bytes=64)
+                    scales[key] = work.tile([P, 512], U8, name="ws", tag="ws", bufs=W_BUFS, align_bytes=64)
+                cols = slice(P * unit[2], P * (unit[2] + 1)) if by_rows else slice(0, 512)
+                src = staged[unit][:, 512 * g : 512 * (g + 1)] if by_rows else staged[unit][:]
+                nc.vector.quantize_mx(out=codes[key][:, cols].bitcast(E4M3), scales=scales[key][:, cols], in_=src)
 
         acc = {}
 
         def multiply(t):
             sweep, tok = divmod(t, TOK_TILES)
-            acc[t] = psum.tile([P, 512], F32, name="acc", tag="acc")
+            acc[t] = psum.tile([P, 512], F32, name="acc", tag="acc", bufs=BANKS["acc"])
             x = ("x", tok, 0)
             for g in range(PASSES):
                 w = ("w", sweep, g)
@@ -122,15 +135,20 @@ def tile_biboattention_pa_kernel(
         def norm_stats(t):
             sweep, tok = divmod(t, TOK_TILES)
             squares = work.tile([P, HEADS, HD], BF16, name="squares", tag="squares")
-            for h in range(HEADS):
+            step = HEADS if t < TILES - 1 else LAST_STEP
+            for first in range(0, HEADS, step):
+                for h in range(first, first + step):
+                    nc.scalar.activation(
+                        out=squares[:, h, :],
+                        in_=acc[t][:, HD * h : HD * (h + 1)],
+                        func=ACT.Square,
+                        accum_out=sumsq[:, t, h : h + 1],
+                    )
+                hs = slice(first, first + step)
+                dst = rstd_gain[:, sweep, tok, hs, 0] if sweep < Q_SWEEPS else factor[:, t, hs]
                 nc.scalar.activation(
-                    out=squares[:, h, :],
-                    in_=acc[t][:, HD * h : HD * (h + 1)],
-                    func=ACT.Square,
-                    accum_out=sumsq[:, t, h : h + 1],
+                    out=dst, in_=sumsq[:, t, hs], func=ACT.Abs_reciprocal_sqrt, scale=1.0 / HD, bias=EPS
                 )
-            dst = rstd_gain[:, sweep, tok, :, 0] if sweep < Q_SWEEPS else factor[:, t, :]
-            nc.scalar.activation(out=dst, in_=sumsq[:, t, :], func=ACT.Abs_reciprocal_sqrt, scale=1.0 / HD, bias=EPS)
 
         def apply_gain(t):
             sweep, tok = divmod(t, TOK_TILES)
@@ -143,11 +161,11 @@ def tile_biboattention_pa_kernel(
 
         def rope_terms(t, h):
             sweep, tok = divmod(t, TOK_TILES)
-            if h == 0:
-                terms[t] = work.tile([P, HEADS, 2, HD], F32, name="terms", tag="terms", bufs=4)
+            if h == 0 and t % 2 == 0:
+                terms[t // 2] = work.tile([P, 2, HEADS, 2, HD], F32, name="terms", tag="terms", bufs=3)
             table = tables[0 if sweep < Q_SWEEPS else 1]
             nc.vector.scalar_tensor_tensor(
-                out=terms[t][:, h],
+                out=terms[t // 2][:, t % 2, h],
                 in0=acc[t][:, HD * h : HD * (h + 1)].unsqueeze(1).to_broadcast([P, 2, HD]),
                 scalar=factor[:, t, h : h + 1],
                 in1=table[:, tok % ROWS],
@@ -157,58 +175,59 @@ def tile_biboattention_pa_kernel(
 
         result = {}
 
-        def rope_sum_and_store(t):
+        def rope_sum_and_store(t, engine, count, hs=slice(0, HEADS)):
             sweep, tok = divmod(t, TOK_TILES)
             b, i = divmod(tok, ROWS)
             if i == 0:
                 result[t // ROWS] = work.tile([P, HEADS, ROWS, HD], F32, name="result", tag="result")
             res = result[t // ROWS]
-            engine = nc.vector if t == TILES - 1 else nc.gpsimd
-            for half in range(2):
-                own = slice(HALF * half, HALF * (half + 1))
-                other = slice(HALF * (1 - half), HALF * (2 - half))
-                engine.tensor_tensor(
-                    out=res[:, :, i, own], in0=terms[t][:, :, 0, own], in1=terms[t][:, :, 1, other], op=ALU.add
-                )
+            rows = slice(i, i + count)
+            pair = terms[t // 2][:, t % 2 : t % 2 + count, hs].rearrange("p i h w (f d) -> p (i h) w f d", f=2)
+            engine.tensor_tensor(
+                out=res[:, hs, rows, :].rearrange("p h i d -> p i h d"),
+                in0=pair[:, :, 0],
+                in1=pair[:, :, 1, ::-1, :],
+                op=ALU.add,
+            )
             heads = out_0[b, HEADS * sweep : HEADS * (sweep + 1)] if sweep < Q_SWEEPS else out_1[b]
             dst = heads.rearrange("h (p i) d -> p h i d", i=ROWS)
             if t >= TILES - ROWS:
-                nc.sync.dma_start(out=dst[:, :, i], in_=res[:, :, i])
-            elif i == ROWS - 1:
+                nc.sync.dma_start(out=dst[:, hs, rows], in_=res[:, hs, rows])
+            elif i + count == ROWS:
                 nc.sync.dma_start(out=dst, in_=res[:])
 
         xs = [("x", a, 0) for a in range(TOK_TILES)]
         ws = [[("w", j, g) for g in range(PASSES)] for j in range(SWEEPS)]
-        head = [xs[0]] + ws[0] + xs[1:3]
+        order = [xs[0]] + ws[0] + xs[1:] + [unit for w in ws[1:] for unit in w]
+        gaps = list(range(15, 30, 2))
+        head = order[: len(order) - len(gaps)]
         after = {t: [] for t in range(-1, TILES)}
-        for n, unit in enumerate(xs[3:]):
-            after[n].append(unit)
-        for g, t in enumerate((0, 2, 4, 5)):
-            after[t].append(ws[1][g])
-        for j in range(2, SWEEPS):
-            for g in range(PASSES):
-                after[TOK_TILES * (j - 1) - 1 + 2 * g].append(ws[j][g])
+        for t, unit in zip(gaps, order[len(head) :]):
+            after[t].append(unit)
 
-        for unit in head:
-            load(unit)
         cos_sb = keep.tile([P, ROWS, HD], BF16, name="cos_sb")
         sin_sb = keep.tile([P, ROWS, HD], BF16, name="sin_sb")
-        nc.sync.dma_start(out=cos_sb[:], in_=cos.rearrange("(p i) d -> p i d", i=ROWS))
-        nc.sync.dma_start(out=sin_sb[:], in_=sin.rearrange("(p i) d -> p i d", i=ROWS))
-        for t in range(TILES):
-            for unit in after[t]:
-                load(unit)
+        for n, unit in enumerate(order[:RAW_BUFS]):
+            if n == len(head):
+                nc.sync.dma_start(out=cos_sb[:], in_=cos.rearrange("(p i) d -> p i d", i=ROWS))
+                nc.sync.dma_start(out=sin_sb[:], in_=sin.rearrange("(p i) d -> p i d", i=ROWS))
+            load(unit)
 
         for unit in head:
-            transpose_and_stage([unit])
+            transpose_and_stage([unit], tag="acc")
             quantize(unit)
+            for later in order[order.index(unit) + RAW_BUFS :][:1]:
+                load(later)
+            if unit == ws[0][-1]:
+                spread = psum.tile([P, 512], F32, name="spread", tag="tr", bufs=BANKS["tr"])
+                nc.tensor.matmul(out=spread[:, 0 : 2 * HD + NH], lhsT=ones[:], rhs=vec[:], start=True, stop=True)
+                params = keep.tile([P, 2 * HD + NH], F32, name="params")
+                nc.vector.tensor_copy(out=params[:], in_=spread[:, 0 : 2 * HD + NH])
 
-        spread = psum.tile([P, 512], F32, name="spread", tag="acc")
-        nc.tensor.matmul(out=spread[:, 0 : 2 * HD + NH], lhsT=ones[:], rhs=vec[:], start=True, stop=True)
         tables = [keep.tile([P, ROWS, 2, HD], F32, name="table%d" % n) for n in range(2)]
 
         def build_table(n):
-            w = spread[:, HD * n : HD * (n + 1)].unsqueeze(1)
+            w = params[:, HD * n : HD * (n + 1)].unsqueeze(1)
             nc.vector.tensor_tensor(
                 out=tables[n][:, :, 0, :], in0=cos_sb[:], in1=w.to_broadcast([P, ROWS, HD]), op=ALU.mult
             )
@@ -227,7 +246,7 @@ def tile_biboattention_pa_kernel(
                 op1=ALU.mult,
             )
 
-        gain = spread[:, 2 * HD : 2 * HD + NH].rearrange("p (j h) -> p j h", h=HEADS).unsqueeze(2)
+        gain = params[:, 2 * HD : 2 * HD + NH].rearrange("p (j h) -> p j h", h=HEADS).unsqueeze(2)
         nc.vector.tensor_scalar(
             out=rstd_gain[:, :, :, :, 1],
             in0=gain.to_broadcast([P, Q_SWEEPS, TOK_TILES, HEADS]),
@@ -241,19 +260,24 @@ def tile_biboattention_pa_kernel(
             multiply(t)
             transpose_and_stage(after[t], between=lambda: norm_stats(t))
 
+        build_table(1)
         start_tile(0)
         apply_gain(0)
-        build_table(1)
-        for t in range(TILES):
-            more = t + 1 < TILES
-            if more:
-                start_tile(t + 1)
+        last = TILES - 1
+        for t in range(last):
+            start_tile(t + 1)
             for h in range(HEADS):
-                if more and h == HEADS - 1 and not after[t]:
+                if h == HEADS - 1 and not after[t]:
                     apply_gain(t + 1)
                 rope_terms(t, h)
-            rope_sum_and_store(t)
-            if more and after[t]:
+            for unit in after[t]:
+                quantize(unit)
+            if t % 2 == 1:
+                rope_sum_and_store(t - 1, nc.gpsimd, 2)
+            if after[t]:
                 apply_gain(t + 1)
-                for unit in after[t]:
-                    quantize(unit)
+        for h in range(HEADS):
+            rope_terms(last, h)
+        rope_sum_and_store(last - 1, nc.vector, 1)
+        rope_sum_and_store(last, nc.vector, 1, slice(0, 2))
+        rope_sum_and_store(last, nc.vector, 1, slice(2, 4))

@@ -19,19 +19,25 @@ ACT = mybir.ActivationFunctionType
 
 P = 128
 HALF = HD // 2
-PASSES = H // 512
+K_PASS = 512
+PASSES = H // K_PASS
+SLOTS = 4
+SLOT_WORDS = K_PASS // 2
 HEADS = 4
+N_TILE = HEADS * HD
 ROWS = S // P
 TOK_TILES = B * ROWS
-SWEEPS = (NH + NKV) // HEADS
 Q_SWEEPS = NH // HEADS
+SWEEPS = Q_SWEEPS + NKV // HEADS
 TILES = SWEEPS * TOK_TILES
+N_PARAMS = 2 * HD + NH
+
+ROW_SWEEPS = 2
+UNIT_BEHIND = range(7, 28, 2)
+RAW_BUFS = 23
+W_BUFS = 9
 BANKS = {"acc": 6, "tr": 2}
-LAST_STEP = 4
-HEAD_SWEEPS = 3
-W_BUFS = 12
-RAW_BUFS = 22
-SLOT_WORDS = 256
+PAD = 8
 
 
 def tile_biboattention_pa_kernel(
@@ -41,243 +47,227 @@ def tile_biboattention_pa_kernel(
     with ExitStack() as ctx:
         keep = ctx.enter_context(tc.tile_pool(name="keep", bufs=1))
         work = ctx.enter_context(tc.tile_pool(name="work", bufs=3))
-        psum = ctx.enter_context(tc.psum_pool(name="psum", bufs=4))
+        psum = ctx.enter_context(tc.psum_pool(name="psum", bufs=1))
         ctx.enter_context(tc.manual_schedule())
 
         ident = keep.tile([P, P], F32, name="ident")
         make_identity(nc, ident[:])
-        ones = keep.tile([P, P], BF16, name="ones")
-        vec = keep.tile([P, 2 * HD + NH], BF16, name="vec")
-        nc.vector.memset(vec[:], 0.0)
-        nc.vector.memset(ones[:], 1.0)
-        nc.scalar.dma_start(out=vec[0:1, 0:HD], in_=q_norm_w.rearrange("(o d) -> o d", o=1))
-        nc.scalar.dma_start(out=vec[0:1, HD : 2 * HD], in_=k_norm_w.rearrange("(o d) -> o d", o=1))
-        nc.scalar.dma_start(out=vec[0:1, 2 * HD :], in_=ssmax_scale.rearrange("o h a c -> o (h a c)"))
 
-        raw, staged, codes, scales = {}, {}, {}, {}
+        ones = keep.tile([P, P], BF16, name="ones")
+        param_row = keep.tile([P, N_PARAMS], BF16, name="param_row")
+        nc.vector.memset(param_row[:], 0.0)
+        nc.vector.memset(ones[:], 1.0)
+        nc.scalar.dma_start(out=param_row[0:1, 0:HD], in_=q_norm_w.rearrange("(o d) -> o d", o=1))
+        nc.scalar.dma_start(out=param_row[0:1, HD : 2 * HD], in_=k_norm_w.rearrange("(o d) -> o d", o=1))
+        nc.scalar.dma_start(out=param_row[0:1, 2 * HD :], in_=ssmax_scale.rearrange("o h a c -> o (h a c)"))
+
+        x_units = [("x", tok, 0) for tok in range(TOK_TILES)]
+        w_units = [[("w", sweep, part) for part in range(SLOTS)] for sweep in range(SWEEPS)]
+        order = [x_units[0]] + w_units[0] + x_units[1:] + [unit for units in w_units[1:] for unit in units]
+        head = order[: len(order) - len(UNIT_BEHIND)]
+        behind = dict(zip(UNIT_BEHIND, order[len(head) :]))
+
+        raw, staged, x_codes, x_scales, w_codes, w_scales = {}, {}, {}, {}, {}, {}
 
         def load(unit):
-            kind, a, g = unit
-            tile = work.tile([P, 4, 512], BF16, name="raw", tag="raw", bufs=RAW_BUFS)
+            kind, index, part = unit
+            raw[unit] = work.tile([P, SLOTS, K_PASS], BF16, name="raw", tag="raw", bufs=RAW_BUFS)
             if kind == "x":
-                src = hidden_states[a // ROWS].rearrange("(p i) (g k) -> p i g k", i=ROWS, k=512)[:, a % ROWS]
+                batch, i = divmod(index, ROWS)
+                src = hidden_states[batch].rearrange("(p i) (g k) -> p i g k", i=ROWS, k=K_PASS)[:, i]
             else:
-                w = wq[512 * a : 512 * (a + 1)] if a < Q_SWEEPS else wk
-                if a < HEAD_SWEEPS:
-                    src = w[P * g : P * (g + 1)].rearrange("p (g k) -> p g k", k=512)
+                weight = wq[N_TILE * index : N_TILE * (index + 1)] if index < Q_SWEEPS else wk
+                if index < ROW_SWEEPS:
+                    src = weight[P * part : P * (part + 1)].rearrange("p (g k) -> p g k", k=K_PASS)
                 else:
-                    src = w[:, 512 * g : 512 * (g + 1)].rearrange("(r p) k -> p r k", p=P)
-            if unit == ("x", 0, 0):
-                nc.sync.dma_start(out=tile[:, 0:2], in_=src[:, 0:2])
-                nc.sync.dma_start(out=tile[:, 2:4], in_=src[:, 2:4])
-            else:
-                nc.sync.dma_start(out=tile[:], in_=src)
-            raw[unit] = tile
+                    src = weight[:, K_PASS * part : K_PASS * (part + 1)].rearrange("(r p) k -> p r k", p=P)
+            step = SLOTS // 2 if unit == order[0] else SLOTS
+            for first in range(0, SLOTS, step):
+                nc.sync.dma_start(out=raw[unit][:, first : first + step], in_=src[:, first : first + step])
 
-        def transpose_and_stage(units, between=None, tag="tr"):
+        def transpose(unit, tag):
+            words = raw[unit][:].rearrange("p a k -> p (a k)").bitcast(F32)
             banks = []
-            for unit in units:
-                words = raw[unit][:].rearrange("p a k -> p (a k)").bitcast(F32)
-                for pair in range(2):
-                    bank = psum.tile([P, 2, 2, P], F32, name="tr", tag=tag, bufs=BANKS[tag])
-                    for a in range(2):
-                        base = SLOT_WORDS * (2 * pair + a)
-                        for u in range(2):
-                            nc.tensor.transpose(bank[:, a, u, :], words[:, base + u : base + SLOT_WORDS : 2], ident[:])
-                    banks.append((unit, pair, bank))
-            if between is not None:
-                between()
-            for unit, pair, bank in banks:
-                if pair == 0:
-                    staged[unit] = work.tile([P, 4 * 512], BF16, name="staged", tag="staged", bufs=4, align_bytes=64)
-                dst = staged[unit][:].bitcast(F32).rearrange("p (a c u) -> p a c u", a=4, u=2)
+            for pair in range(SLOTS // 2):
+                bank = psum.tile([P, 2, 2, P], F32, name="turned", tag=tag, bufs=BANKS[tag])
+                for a in range(2):
+                    base = SLOT_WORDS * (2 * pair + a)
+                    for u in range(2):
+                        nc.tensor.transpose(bank[:, a, u, :], words[:, base + u : base + SLOT_WORDS : 2], ident[:])
+                banks.append(bank)
+            return banks
+
+        def stage(unit, banks):
+            staged[unit] = work.tile([P, SLOTS * K_PASS], BF16, name="staged", tag="staged", bufs=4, align_bytes=64)
+            dst = staged[unit][:].bitcast(F32).rearrange("p (a c u) -> p a c u", a=SLOTS, u=2)
+            for pair, bank in enumerate(banks):
                 nc.scalar.copy(out=dst[:, 2 * pair : 2 * pair + 2], in_=bank[:].rearrange("p a u c -> p a c u"))
 
         def quantize(unit):
-            if unit[0] == "x":
-                codes[unit] = keep.tile([P, 512], U32, name="xc%d" % unit[1], align_bytes=64)
-                scales[unit] = keep.tile([P, 512], U8, name="xs%d" % unit[1], align_bytes=64)
-                nc.vector.quantize_mx(out=codes[unit][:].bitcast(E5M2), scales=scales[unit][:], in_=staged[unit][:])
+            kind, index, part = unit
+            if kind == "x":
+                x_codes[index] = keep.tile([P, PASSES * P], U32, name="x_codes%d" % index, align_bytes=64)
+                x_scales[index] = keep.tile([P, PASSES * P], U8, name="x_scales%d" % index, align_bytes=64)
+                nc.vector.quantize_mx(
+                    out=x_codes[index][:].bitcast(E5M2), scales=x_scales[index][:], in_=staged[unit][:]
+                )
                 return
-            by_rows = unit[1] < HEAD_SWEEPS
-            for g in range(PASSES) if by_rows else [unit[2]]:
-                key = ("w", unit[1], g)
-                if key not in codes:
-                    codes[key] = work.tile([P, 512], U32, name="wc", tag="wc", bufs=W_BUFS, align_bytes=64)
-                    scales[key] = work.tile([P, 512], U8, name="ws", tag="ws", bufs=W_BUFS, align_bytes=64)
-                cols = slice(P * unit[2], P * (unit[2] + 1)) if by_rows else slice(0, 512)
-                src = staged[unit][:, 512 * g : 512 * (g + 1)] if by_rows else staged[unit][:]
-                nc.vector.quantize_mx(out=codes[key][:, cols].bitcast(E4M3), scales=scales[key][:, cols], in_=src)
+            by_rows = index < ROW_SWEEPS
+            for g in range(PASSES) if by_rows else [part]:
+                key = (index, g)
+                if key not in w_codes:
+                    w_codes[key] = work.tile([P, N_TILE], U32, name="w_codes", bufs=W_BUFS, align_bytes=64)
+                    w_scales[key] = work.tile([P, N_TILE], U8, name="w_scales", bufs=W_BUFS, align_bytes=64)
+                cols = slice(P * part, P * (part + 1)) if by_rows else slice(0, N_TILE)
+                src = staged[unit][:, K_PASS * g : K_PASS * (g + 1)] if by_rows else staged[unit][:]
+                nc.vector.quantize_mx(out=w_codes[key][:, cols].bitcast(E4M3), scales=w_scales[key][:, cols], in_=src)
 
-        acc = {}
+        acc, terms, result = {}, {}, {}
+        sumsq = keep.tile([P, TILES, HEADS], F32, name="sumsq")
+        rstd_gain = keep.tile([P, Q_SWEEPS, TOK_TILES, HEADS, 2], F32, name="rstd_gain")
+        factor = keep.tile([P, TILES, PAD], F32, name="factor")
+        params = keep.tile([P, N_PARAMS], F32, name="params")
+        tables = [keep.tile([P, ROWS, 2, HD], F32, name="table%d" % n) for n in range(2)]
+        cos_sb = keep.tile([P, ROWS, HD], BF16, name="cos_sb")
+        sin_sb = keep.tile([P, ROWS, HD], BF16, name="sin_sb")
+        sin_swapped = keep.tile([P, ROWS, HD], BF16, name="sin_swapped")
 
         def multiply(t):
             sweep, tok = divmod(t, TOK_TILES)
-            acc[t] = psum.tile([P, 512], F32, name="acc", tag="acc", bufs=BANKS["acc"])
-            x = ("x", tok, 0)
+            acc[t] = psum.tile([P, N_TILE], F32, name="acc", tag="acc", bufs=BANKS["acc"])
             for g in range(PASSES):
-                w = ("w", sweep, g)
                 cols = slice(P * g, P * (g + 1))
                 nc.tensor.matmul_mx(
                     out=acc[t][:],
-                    lhsT=codes[x][:, cols].bitcast(E5M2),
-                    lhsT_scale=scales[x][:, cols],
-                    rhs=codes[w][:].bitcast(E4M3),
-                    rhs_scale=scales[w][:],
+                    lhsT=x_codes[tok][:, cols].bitcast(E5M2),
+                    lhsT_scale=x_scales[tok][:, cols],
+                    rhs=w_codes[(sweep, g)][:].bitcast(E4M3),
+                    rhs_scale=w_scales[(sweep, g)][:],
                     start=(g == 0),
                     stop=(g == PASSES - 1),
                 )
 
-        sumsq = keep.tile([P, TILES, HEADS], F32, name="sumsq")
-        rstd_gain = keep.tile([P, Q_SWEEPS, TOK_TILES, HEADS, 2], F32, name="rstd_gain")
-        factor = keep.tile([P, TILES, HEADS], F32, name="factor")
-
         def norm_stats(t):
             sweep, tok = divmod(t, TOK_TILES)
-            squares = work.tile([P, HEADS, HD], BF16, name="squares", tag="squares")
-            step = HEADS if t < TILES - 1 else LAST_STEP
-            for first in range(0, HEADS, step):
-                for h in range(first, first + step):
-                    nc.scalar.activation(
-                        out=squares[:, h, :],
-                        in_=acc[t][:, HD * h : HD * (h + 1)],
-                        func=ACT.Square,
-                        accum_out=sumsq[:, t, h : h + 1],
-                    )
-                hs = slice(first, first + step)
-                dst = rstd_gain[:, sweep, tok, hs, 0] if sweep < Q_SWEEPS else factor[:, t, hs]
+            squares = work.tile([P, HEADS, HD], BF16, name="squares")
+            for h in range(HEADS):
                 nc.scalar.activation(
-                    out=dst, in_=sumsq[:, t, hs], func=ACT.Abs_reciprocal_sqrt, scale=1.0 / HD, bias=EPS
+                    out=squares[:, h, :],
+                    in_=acc[t][:, HD * h : HD * (h + 1)],
+                    func=ACT.Square,
+                    accum_out=sumsq[:, t, h : h + 1],
                 )
+            dst = rstd_gain[:, sweep, tok, :, 0] if sweep < Q_SWEEPS else factor[:, t, 0:HEADS]
+            nc.scalar.activation(out=dst, in_=sumsq[:, t, :], func=ACT.Abs_reciprocal_sqrt, scale=1.0 / HD, bias=EPS)
+
+        def start_tile(t):
+            multiply(t)
+            banks = transpose(behind[t], "tr") if t in behind else None
+            norm_stats(t)
+            if t in behind:
+                stage(behind[t], banks)
 
         def apply_gain(t):
             sweep, tok = divmod(t, TOK_TILES)
-            if sweep < Q_SWEEPS:
-                nc.vector.tensor_reduce(
-                    out=factor[:, t, :], in_=rstd_gain[:, sweep, tok], axis=mybir.AxisListType.X, op=ALU.mult
-                )
-
-        terms = {}
+            if sweep >= Q_SWEEPS:
+                return
+            both, dst = rstd_gain[:, sweep, tok], factor[:, t, 0:HEADS]
+            if t % 2 == 0:
+                nc.gpsimd.tensor_tensor(out=dst, in0=both[:, :, 0], in1=both[:, :, 1], op=ALU.mult)
+            else:
+                nc.vector.tensor_reduce(out=dst, in_=both, axis=mybir.AxisListType.X, op=ALU.mult)
 
         def rope_terms(t, h):
             sweep, tok = divmod(t, TOK_TILES)
             if h == 0 and t % 2 == 0:
-                terms[t // 2] = work.tile([P, 2, HEADS, 2, HD], F32, name="terms", tag="terms", bufs=3)
-            table = tables[0 if sweep < Q_SWEEPS else 1]
+                terms[t // 2] = work.tile([P, 2, HEADS, 2, HD], F32, name="terms")
             nc.vector.scalar_tensor_tensor(
                 out=terms[t // 2][:, t % 2, h],
                 in0=acc[t][:, HD * h : HD * (h + 1)].unsqueeze(1).to_broadcast([P, 2, HD]),
                 scalar=factor[:, t, h : h + 1],
-                in1=table[:, tok % ROWS],
+                in1=tables[sweep // Q_SWEEPS][:, tok % ROWS],
                 op0=ALU.mult,
                 op1=ALU.mult,
             )
 
-        result = {}
-
-        def rope_sum_and_store(t, engine, count, hs=slice(0, HEADS)):
+        def rope_sum_and_store(t, count, heads, engine):
             sweep, tok = divmod(t, TOK_TILES)
-            b, i = divmod(tok, ROWS)
+            batch, i = divmod(tok, ROWS)
             if i == 0:
-                result[t // ROWS] = work.tile([P, HEADS, ROWS, HD], F32, name="result", tag="result")
+                result[t // ROWS] = work.tile([P, HEADS, ROWS, HD], F32, name="result")
             res = result[t // ROWS]
             rows = slice(i, i + count)
-            pair = terms[t // 2][:, t % 2 : t % 2 + count, hs].rearrange("p i h w (f d) -> p (i h) w f d", f=2)
+            both = terms[t // 2][:, t % 2 : t % 2 + count, heads].rearrange("p i h w (f d) -> p (i h) w f d", f=2)
             engine.tensor_tensor(
-                out=res[:, hs, rows, :].rearrange("p h i d -> p i h d"),
-                in0=pair[:, :, 0],
-                in1=pair[:, :, 1, ::-1, :],
+                out=res[:, heads, rows, :].rearrange("p h i d -> p i h d"),
+                in0=both[:, :, 0],
+                in1=both[:, :, 1, ::-1, :],
                 op=ALU.add,
             )
-            heads = out_0[b, HEADS * sweep : HEADS * (sweep + 1)] if sweep < Q_SWEEPS else out_1[b]
-            dst = heads.rearrange("h (p i) d -> p h i d", i=ROWS)
+            out = out_0[batch, HEADS * sweep : HEADS * (sweep + 1)] if sweep < Q_SWEEPS else out_1[batch]
+            dst = out.rearrange("h (p i) d -> p h i d", i=ROWS)
             if t >= TILES - ROWS:
-                nc.sync.dma_start(out=dst[:, hs, rows], in_=res[:, hs, rows])
+                nc.sync.dma_start(out=dst[:, heads, rows], in_=res[:, heads, rows])
             elif i + count == ROWS:
                 nc.sync.dma_start(out=dst, in_=res[:])
 
-        xs = [("x", a, 0) for a in range(TOK_TILES)]
-        ws = [[("w", j, g) for g in range(PASSES)] for j in range(SWEEPS)]
-        order = [xs[0]] + ws[0] + xs[1:] + [unit for w in ws[1:] for unit in w]
-        gaps = list(range(15, 30, 2))
-        head = order[: len(order) - len(gaps)]
-        after = {t: [] for t in range(-1, TILES)}
-        for t, unit in zip(gaps, order[len(head) :]):
-            after[t].append(unit)
+        def spread_params():
+            spread = psum.tile([P, N_PARAMS], F32, name="spread", tag="tr", bufs=BANKS["tr"])
+            nc.tensor.matmul(out=spread[:], lhsT=ones[:], rhs=param_row[:], start=True, stop=True)
+            nc.vector.tensor_copy(out=params[:], in_=spread[:])
+            gain = params[:, 2 * HD :].rearrange("p (j h) -> p j h", h=HEADS).unsqueeze(2)
+            nc.vector.tensor_scalar(
+                out=rstd_gain[:, :, :, :, 1],
+                in0=gain.to_broadcast([P, Q_SWEEPS, TOK_TILES, HEADS]),
+                scalar1=math.log(S),
+                scalar2=None,
+                op0=ALU.mult,
+            )
 
-        cos_sb = keep.tile([P, ROWS, HD], BF16, name="cos_sb")
-        sin_sb = keep.tile([P, ROWS, HD], BF16, name="sin_sb")
+        def build_table(n, engine):
+            w = params[:, HD * n : HD * (n + 1)].unsqueeze(1).to_broadcast([P, ROWS, HD])
+            engine.tensor_tensor(out=tables[n][:, :, 0, :], in0=cos_sb[:], in1=w, op=ALU.mult)
+            engine.tensor_tensor(out=tables[n][:, :, 1, :], in0=sin_swapped[:], in1=w, op=ALU.mult)
+
         for n, unit in enumerate(order[:RAW_BUFS]):
             if n == len(head):
                 nc.sync.dma_start(out=cos_sb[:], in_=cos.rearrange("(p i) d -> p i d", i=ROWS))
                 nc.sync.dma_start(out=sin_sb[:], in_=sin.rearrange("(p i) d -> p i d", i=ROWS))
             load(unit)
 
-        for unit in head:
-            transpose_and_stage([unit], tag="acc")
+        for n, unit in enumerate(head):
+            stage(unit, transpose(unit, "acc"))
             quantize(unit)
-            for later in order[order.index(unit) + RAW_BUFS :][:1]:
-                load(later)
-            if unit == ws[0][-1]:
-                spread = psum.tile([P, 512], F32, name="spread", tag="tr", bufs=BANKS["tr"])
-                nc.tensor.matmul(out=spread[:, 0 : 2 * HD + NH], lhsT=ones[:], rhs=vec[:], start=True, stop=True)
-                params = keep.tile([P, 2 * HD + NH], F32, name="params")
-                nc.vector.tensor_copy(out=params[:], in_=spread[:, 0 : 2 * HD + NH])
+            if n + RAW_BUFS < len(order):
+                load(order[n + RAW_BUFS])
+            if unit == w_units[0][-1]:
+                spread_params()
 
-        tables = [keep.tile([P, ROWS, 2, HD], F32, name="table%d" % n) for n in range(2)]
-
-        def build_table(n):
-            w = params[:, HD * n : HD * (n + 1)].unsqueeze(1)
-            nc.vector.tensor_tensor(
-                out=tables[n][:, :, 0, :], in0=cos_sb[:], in1=w.to_broadcast([P, ROWS, HD]), op=ALU.mult
-            )
-            nc.vector.tensor_tensor(
-                out=tables[n][:, :, 1, 0:HALF],
-                in0=sin_sb[:, :, HALF:HD],
-                in1=w[:, :, 0:HALF].to_broadcast([P, ROWS, HALF]),
-                op=ALU.mult,
-            )
-            nc.vector.scalar_tensor_tensor(
-                out=tables[n][:, :, 1, HALF:HD],
-                in0=sin_sb[:, :, 0:HALF],
-                scalar=-1.0,
-                in1=w[:, :, HALF:HD].to_broadcast([P, ROWS, HALF]),
-                op0=ALU.mult,
-                op1=ALU.mult,
-            )
-
-        gain = params[:, 2 * HD : 2 * HD + NH].rearrange("p (j h) -> p j h", h=HEADS).unsqueeze(2)
+        nc.vector.tensor_copy(out=sin_swapped[:, :, 0:HALF], in_=sin_sb[:, :, HALF:HD])
         nc.vector.tensor_scalar(
-            out=rstd_gain[:, :, :, :, 1],
-            in0=gain.to_broadcast([P, Q_SWEEPS, TOK_TILES, HEADS]),
-            scalar1=math.log(S),
-            scalar2=None,
-            op0=ALU.mult,
+            out=sin_swapped[:, :, HALF:HD], in0=sin_sb[:, :, 0:HALF], scalar1=-1.0, scalar2=None, op0=ALU.mult
         )
-        build_table(0)
+        build_table(0, nc.vector)
 
-        def start_tile(t):
-            multiply(t)
-            transpose_and_stage(after[t], between=lambda: norm_stats(t))
-
-        build_table(1)
+        all_heads = slice(0, HEADS)
         start_tile(0)
+        start_tile(1)
         apply_gain(0)
-        last = TILES - 1
-        for t in range(last):
-            start_tile(t + 1)
-            for h in range(HEADS):
-                if h == HEADS - 1 and not after[t]:
-                    apply_gain(t + 1)
-                rope_terms(t, h)
-            for unit in after[t]:
-                quantize(unit)
-            if t % 2 == 1:
-                rope_sum_and_store(t - 1, nc.gpsimd, 2)
-            if after[t]:
-                apply_gain(t + 1)
-        for h in range(HEADS):
-            rope_terms(last, h)
-        rope_sum_and_store(last - 1, nc.vector, 1)
-        rope_sum_and_store(last, nc.vector, 1, slice(0, 2))
-        rope_sum_and_store(last, nc.vector, 1, slice(2, 4))
+        build_table(1, nc.gpsimd)
+        for even in range(0, TILES, 2):
+            for t in (even, even + 1):
+                for h in range(HEADS):
+                    if t == even and h == HEADS - 1:
+                        apply_gain(even + 1)
+                    rope_terms(t, h)
+                if t in behind:
+                    quantize(behind[t])
+                if t + 2 < TILES:
+                    start_tile(t + 2)
+            if even + 2 < TILES:
+                apply_gain(even + 2)
+                rope_sum_and_store(even, 2, all_heads, nc.gpsimd)
+
+        rope_sum_and_store(TILES - 2, 1, all_heads, nc.vector)
+        rope_sum_and_store(TILES - 1, 1, slice(0, HEADS // 2), nc.vector)
+        rope_sum_and_store(TILES - 1, 1, slice(HEADS // 2, HEADS), nc.vector)

@@ -32,10 +32,10 @@ SWEEPS = Q_SWEEPS + NKV // HEADS
 TILES = SWEEPS * TOK_TILES
 N_PARAMS = 2 * HD + NH
 
-ROW_SWEEPS = 2
-UNIT_BEHIND = range(7, 28, 2)
+ROW_SWEEPS = 1
+UNIT_BEHIND = range(3, 30, 2)
 RAW_BUFS = 23
-W_BUFS = 9
+W_BUFS = 2 * PASSES
 BANKS = {"acc": 6, "tr": 2}
 PAD = 8
 
@@ -98,7 +98,7 @@ def tile_biboattention_pa_kernel(
             return banks
 
         def stage(unit, banks):
-            staged[unit] = work.tile([P, SLOTS * K_PASS], BF16, name="staged", tag="staged", bufs=4, align_bytes=64)
+            staged[unit] = work.tile([P, SLOTS * K_PASS], BF16, name="staged", tag="staged", bufs=4, align_bytes=256)
             dst = staged[unit][:].bitcast(F32).rearrange("p (a c u) -> p a c u", a=SLOTS, u=2)
             for pair, bank in enumerate(banks):
                 nc.scalar.copy(out=dst[:, 2 * pair : 2 * pair + 2], in_=bank[:].rearrange("p a u c -> p a c u"))
@@ -106,8 +106,8 @@ def tile_biboattention_pa_kernel(
         def quantize(unit):
             kind, index, part = unit
             if kind == "x":
-                x_codes[index] = keep.tile([P, PASSES * P], U32, name="x_codes%d" % index, align_bytes=64)
-                x_scales[index] = keep.tile([P, PASSES * P], U8, name="x_scales%d" % index, align_bytes=64)
+                x_codes[index] = keep.tile([P, PASSES * P], U32, name="x_codes%d" % index, align_bytes=256)
+                x_scales[index] = keep.tile([P, PASSES * P], U8, name="x_scales%d" % index, align_bytes=256)
                 nc.vector.quantize_mx(
                     out=x_codes[index][:].bitcast(E5M2), scales=x_scales[index][:], in_=staged[unit][:]
                 )
@@ -116,8 +116,8 @@ def tile_biboattention_pa_kernel(
             for g in range(PASSES) if by_rows else [part]:
                 key = (index, g)
                 if key not in w_codes:
-                    w_codes[key] = work.tile([P, N_TILE], U32, name="w_codes", bufs=W_BUFS, align_bytes=64)
-                    w_scales[key] = work.tile([P, N_TILE], U8, name="w_scales", bufs=W_BUFS, align_bytes=64)
+                    w_codes[key] = work.tile([P, N_TILE], U32, name="w_codes", bufs=W_BUFS, align_bytes=256)
+                    w_scales[key] = work.tile([P, N_TILE], U8, name="w_scales", bufs=W_BUFS, align_bytes=256)
                 cols = slice(P * part, P * (part + 1)) if by_rows else slice(0, N_TILE)
                 src = staged[unit][:, K_PASS * g : K_PASS * (g + 1)] if by_rows else staged[unit][:]
                 nc.vector.quantize_mx(out=w_codes[key][:, cols].bitcast(E4M3), scales=w_scales[key][:, cols], in_=src)

import math
from contextlib import ExitStack

import concourse.mybir as mybir
from concourse.masks import make_identity

B, S, H, NH, NKV, HD = 2, 512, 2048, 16, 4, 128
EPS = 1e-6
FLOPS = 2 * B * S * H * (NH + NKV) * HD

F32 = mybir.dt.float32
BF16 = mybir.dt.bfloat16
U32 = mybir.dt.uint32
U8 = mybir.dt.uint8
E5M2 = mybir.dt.float8_e5m2_x4
E4M3 = mybir.dt.float8_e4m3fn_x4
ALU = mybir.AluOpType
ACT = mybir.ActivationFunctionType

P = 128
HALF = HD // 2
K_PASS = 512
PASSES = H // K_PASS
SLOTS = 4
SLOT_WORDS = K_PASS // 2
HEADS = 4
N_TILE = HEADS * HD
ROWS = S // P
TOK_TILES = B * ROWS
Q_SWEEPS = NH // HEADS
SWEEPS = Q_SWEEPS + NKV // HEADS
TILES = SWEEPS * TOK_TILES
N_PARAMS = 2 * HD + NH

ROW_SWEEPS = 1
UNIT_BEHIND = range(3, 30, 2)
RAW_BUFS = 23
W_BUFS = 2 * PASSES
BANKS = {"acc": 6, "tr": 2}
PAD = 8


def tile_biboattention_pa_kernel(
    tc, hidden_states, cos, sin, wq, wk, q_norm_w, k_norm_w, ssmax_scale, out_0, out_1
):
    nc = tc.nc
    with ExitStack() as ctx:
        keep = ctx.enter_context(tc.tile_pool(name="keep", bufs=1))
        work = ctx.enter_context(tc.tile_pool(name="work", bufs=3))
        psum = ctx.enter_context(tc.psum_pool(name="psum", bufs=1))
        ctx.enter_context(tc.manual_schedule())

        ident = keep.tile([P, P], F32, name="ident")
        make_identity(nc, ident[:])

        ones = keep.tile([P, P], BF16, name="ones")
        param_row = keep.tile([P, N_PARAMS], BF16, name="param_row")
        nc.vector.memset(param_row[:], 0.0)
        nc.vector.memset(ones[:], 1.0)
        nc.scalar.dma_start(out=param_row[0:1, 0:HD], in_=q_norm_w.rearrange("(o d) -> o d", o=1))
        nc.scalar.dma_start(out=param_row[0:1, HD : 2 * HD], in_=k_norm_w.rearrange("(o d) -> o d", o=1))
        nc.scalar.dma_start(out=param_row[0:1, 2 * HD :], in_=ssmax_scale.rearrange("o h a c -> o (h a c)"))

        x_units = [("x", tok, 0) for tok in range(TOK_TILES)]
        w_units = [[("w", sweep, part) for part in range(SLOTS)] for sweep in range(SWEEPS)]
        order = [x_units[0]] + w_units[0] + x_units[1:] + [unit for units in w_units[1:] for unit in units]
        head = order[: len(order) - len(UNIT_BEHIND)]
        behind = dict(zip(UNIT_BEHIND, order[len(head) :]))

        raw, staged, x_codes, x_scales, w_codes, w_scales = {}, {}, {}, {}, {}, {}

        def load(unit):
            kind, index, part = unit
            raw[unit] = work.tile([P, SLOTS, K_PASS], BF16, name="raw", tag="raw", bufs=RAW_BUFS)
            if kind == "x":
                batch, i = divmod(index, ROWS)
                src = hidden_states[batch].rearrange("(p i) (g k) -> p i g k", i=ROWS, k=K_PASS)[:, i]
            else:
                weight = wq[N_TILE * index : N_TILE * (index + 1)] if index < Q_SWEEPS else wk
                if index < ROW_SWEEPS:
                    src = weight[P * part : P * (part + 1)].rearrange("p (g k) -> p g k", k=K_PASS)
                else:
                    src = weight[:, K_PASS * part : K_PASS * (part + 1)].rearrange("(r p) k -> p r k", p=P)
            step = SLOTS // 2 if unit == order[0] else SLOTS
            for first in range(0, SLOTS, step):
                nc.sync.dma_start(out=raw[unit][:, first : first + step], in_=src[:, first : first + step])

        def transpose(unit, tag):
            words = raw[unit][:].rearrange("p a k -> p (a k)").bitcast(F32)
            banks = []
            for pair in range(SLOTS // 2):
                bank = psum.tile([P, 2, 2, P], F32, name="turned", tag=tag, bufs=BANKS[tag])
                for a in range(2):
                    base = SLOT_WORDS * (2 * pair + a)
                    for u in range(2):
                        nc.tensor.transpose(bank[:, a, u, :], words[:, base + u : base + SLOT_WORDS : 2], ident[:])
                banks.append(bank)
            return banks

        def stage(unit, banks):
            staged[unit] = work.tile([P, SLOTS * K_PASS], BF16, name="staged", tag="staged", bufs=4, align_bytes=256)
            dst = staged[unit][:].bitcast(F32).rearrange("p (a c u) -> p a c u", a=SLOTS, u=2)
            for pair, bank in enumerate(banks):
                nc.scalar.copy(out=dst[:, 2 * pair : 2 * pair + 2], in_=bank[:].rearrange("p a u c -> p a c u"))

        def quantize(unit):
            kind, index, part = unit
            if kind == "x":
                x_codes[index] = keep.tile([P, PASSES * P], U32, name="x_codes%d" % index, align_bytes=256)
                x_scales[index] = keep.tile([P, PASSES * P], U8, name="x_scales%d" % index, align_bytes=256)
                nc.vector.quantize_mx(
                    out=x_codes[index][:].bitcast(E5M2), scales=x_scales[index][:], in_=staged[unit][:]
                )
                return
            by_rows = index < ROW_SWEEPS
            for g in range(PASSES) if by_rows else [part]:
                key = (index, g)
                if key not in w_codes:
                    w_codes[key] = work.tile([P, N_TILE], U32, name="w_codes", bufs=W_BUFS, align_bytes=256)
                    w_scales[key] = work.tile([P, N_TILE], U8, name="w_scales", bufs=W_BUFS, align_bytes=256)
                cols = slice(P * part, P * (part + 1)) if by_rows else slice(0, N_TILE)
                src = staged[unit][:, K_PASS * g : K_PASS * (g + 1)] if by_rows else staged[unit][:]
                nc.vector.quantize_mx(out=w_codes[key][:, cols].bitcast(E4M3), scales=w_scales[key][:, cols], in_=src)

        acc, terms, result = {}, {}, {}
        sumsq = keep.tile([P, TILES, HEADS], F32, name="sumsq")
        rstd_gain = keep.tile([P, Q_SWEEPS, TOK_TILES, HEADS, 2], F32, name="rstd_gain")
        factor = keep.tile([P, TILES, PAD], F32, name="factor")
        params = keep.tile([P, N_PARAMS], F32, name="params")
        tables = [keep.tile([P, ROWS, 2, HD], F32, name="table%d" % n) for n in range(2)]
        cos_sb = keep.tile([P, ROWS, HD], BF16, name="cos_sb")
        sin_sb = keep.tile([P, ROWS, HD], BF16, name="sin_sb")
        sin_swapped = keep.tile([P, ROWS, HD], BF16, name="sin_swapped")

        def multiply(t):
            sweep, tok = divmod(t, TOK_TILES)
            acc[t] = psum.tile([P, N_TILE], F32, name="acc", tag="acc", bufs=BANKS["acc"])
            for g in range(PASSES):
                cols = slice(P * g, P * (g + 1))
                nc.tensor.matmul_mx(
                    out=acc[t][:],
                    lhsT=x_codes[tok][:, cols].bitcast(E5M2),
                    lhsT_scale=x_scales[tok][:, cols],
                    rhs=w_codes[(sweep, g)][:].bitcast(E4M3),
                    rhs_scale=w_scales[(sweep, g)][:],
                    start=(g == 0),
                    stop=(g == PASSES - 1),
                )

        def norm_stats(t):
            sweep, tok = divmod(t, TOK_TILES)
            squares = work.tile([P, HEADS, HD], BF16, name="squares")
            for h in range(HEADS):
                nc.scalar.activation(
                    out=squares[:, h, :],
                    in_=acc[t][:, HD * h : HD * (h + 1)],
                    func=ACT.Square,
                    accum_out=sumsq[:, t, h : h + 1],
                )
            dst = rstd_gain[:, sweep, tok, :, 0] if sweep < Q_SWEEPS else factor[:, t, 0:HEADS]
            nc.scalar.activation(out=dst, in_=sumsq[:, t, :], func=ACT.Abs_reciprocal_sqrt, scale=1.0 / HD, bias=EPS)

        def start_tile(t):
            multiply(t)
            banks = transpose(behind[t], "tr") if t in behind else None
            norm_stats(t)
            if t in behind:
                stage(behind[t], banks)

        def apply_gain(t):
            sweep, tok = divmod(t, TOK_TILES)
            if sweep >= Q_SWEEPS:
                return
            both, dst = rstd_gain[:, sweep, tok], factor[:, t, 0:HEADS]
            if t % 2 == 0:
                nc.gpsimd.tensor_tensor(out=dst, in0=both[:, :, 0], in1=both[:, :, 1], op=ALU.mult)
            else:
                nc.vector.tensor_reduce(out=dst, in_=both, axis=mybir.AxisListType.X, op=ALU.mult)

        def rope_terms(t, h):
            sweep, tok = divmod(t, TOK_TILES)
            if h == 0 and t % 2 == 0:
                terms[t // 2] = work.tile([P, 2, HEADS, 2, HD], F32, name="terms")
            nc.vector.scalar_tensor_tensor(
                out=terms[t // 2][:, t % 2, h],
                in0=acc[t][:, HD * h : HD * (h + 1)].unsqueeze(1).to_broadcast([P, 2, HD]),
                scalar=factor[:, t, h : h + 1],
                in1=tables[sweep // Q_SWEEPS][:, tok % ROWS],
                op0=ALU.mult,
                op1=ALU.mult,
            )

        def rope_sum_and_store(t, count, heads, engine):
            sweep, tok = divmod(t, TOK_TILES)
            batch, i = divmod(tok, ROWS)
            if i == 0:
                result[t // ROWS] = work.tile([P, HEADS, ROWS, HD], F32, name="result")
            res = result[t // ROWS]
            rows = slice(i, i + count)
            both = terms[t // 2][:, t % 2 : t % 2 + count, heads].rearrange("p i h w (f d) -> p (i h) w f d", f=2)
            engine.tensor_tensor(
                out=res[:, heads, rows, :].rearrange("p h i d -> p i h d"),
                in0=both[:, :, 0],
                in1=both[:, :, 1, ::-1, :],
                op=ALU.add,
            )
            out = out_0[batch, HEADS * sweep : HEADS * (sweep + 1)] if sweep < Q_SWEEPS else out_1[batch]
            dst = out.rearrange("h (p i) d -> p h i d", i=ROWS)
            if t >= TILES - ROWS:
                nc.sync.dma_start(out=dst[:, heads, rows], in_=res[:, heads, rows])
            elif i + count == ROWS:
                nc.sync.dma_start(out=dst, in_=res[:])

        def spread_params():
            spread = psum.tile([P, N_PARAMS], F32, name="spread", tag="tr", bufs=BANKS["tr"])
            nc.tensor.matmul(out=spread[:], lhsT=ones[:], rhs=param_row[:], start=True, stop=True)
            nc.vector.tensor_copy(out=params[:], in_=spread[:])
            gain = params[:, 2 * HD :].rearrange("p (j h) -> p j h", h=HEADS).unsqueeze(2)
            nc.vector.tensor_scalar(
                out=rstd_gain[:, :, :, :, 1],
                in0=gain.to_broadcast([P, Q_SWEEPS, TOK_TILES, HEADS]),
                scalar1=math.log(S),
                scalar2=None,
                op0=ALU.mult,
            )

        def build_table(n, engine):
            w = params[:, HD * n : HD * (n + 1)].unsqueeze(1).to_broadcast([P, ROWS, HD])
            engine.tensor_tensor(out=tables[n][:, :, 0, :], in0=cos_sb[:], in1=w, op=ALU.mult)
            engine.tensor_tensor(out=tables[n][:, :, 1, :], in0=sin_swapped[:], in1=w, op=ALU.mult)

        for n, unit in enumerate(order[:RAW_BUFS]):
            if n == len(head):
                nc.sync.dma_start(out=cos_sb[:], in_=cos.rearrange("(p i) d -> p i d", i=ROWS))
                nc.sync.dma_start(out=sin_sb[:], in_=sin.rearrange("(p i) d -> p i d", i=ROWS))
            load(unit)

        for n, unit in enumerate(head):
            stage(unit, transpose(unit, "acc"))
            quantize(unit)
            if n + RAW_BUFS < len(order):
                load(order[n + RAW_BUFS])
            if unit == w_units[0][-1]:
                spread_params()

        nc.vector.tensor_copy(out=sin_swapped[:, :, 0:HALF], in_=sin_sb[:, :, HALF:HD])
        nc.vector.tensor_scalar(
            out=sin_swapped[:, :, HALF:HD], in0=sin_sb[:, :, 0:HALF], scalar1=-1.0, scalar2=None, op0=ALU.mult
        )
        build_table(0, nc.vector)

        all_heads = slice(0, HEADS)
        start_tile(0)
        start_tile(1)
        apply_gain(0)
        build_table(1, nc.gpsimd)
        for even in range(0, TILES, 2):
            for t in (even, even + 1):
                for h in range(HEADS):
                    if t == even and h == HEADS - 1:
                        apply_gain(even + 1)
                    rope_terms(t, h)
                if t in behind:
                    quantize(behind[t])
                if t + 2 < TILES:
                    start_tile(t + 2)
            if even + 2 < TILES:
                apply_gain(even + 2)
                rope_sum_and_store(even, 2, all_heads, nc.gpsimd)

        rope_sum_and_store(TILES - 2, 1, all_heads, nc.vector)
        rope_sum_and_store(TILES - 1, 1, slice(0, HEADS // 2), nc.vector)
        rope_sum_and_store(TILES - 1, 1, slice(HEADS // 2, HEADS), nc.vector)
